import numpy as np
import ml_dtypes


def mxq(x, axis, fmt="e4m3"):
    dtype, down = {"e4m3": (ml_dtypes.float8_e4m3fn, 7), "e5m2": (ml_dtypes.float8_e5m2, 14)}[fmt]
    v = np.moveaxis(np.asarray(x, np.float32).astype(ml_dtypes.bfloat16).astype(np.float64), axis, -1)
    blocks = v.reshape(v.shape[:-1] + (-1, 32))
    amax = np.abs(blocks).max(-1, keepdims=True)
    byte = np.maximum(np.where(amax > 0, np.frexp(amax)[1] - 1 + 127, 0) - down, 1)
    scale = np.exp2(byte - 127.0)
    codes = (blocks / scale).astype(np.float32).astype(dtype).astype(np.float64)
    return np.moveaxis((codes * scale).reshape(v.shape), -1, axis)


WIDE = False


def mx_kscale(k):
    if not WIDE:
        return np.ones(k)
    levels = np.array([10, -10, 5, -5, 0])
    a = np.random.permutation(np.resize(levels, k // 512 * 4)).reshape(k // 512, 4)
    idx = np.arange(k)
    return np.exp2(a[idx // 512, idx % 128 // 32])


BF16 = ml_dtypes.bfloat16


def bf(x):
    return np.asarray(x, np.float32).astype(BF16)


def f64(x):
    return np.asarray(x).astype(np.float64)


B, S, D, F = 4, 1024, 512, 1024
EPS = 1e-6


def setup_inputs():
    s = mx_kscale(D)
    p = np.exp2(np.round(np.log2(np.mean(1.0 / s**2)) / 2))
    q = np.exp2(np.round(np.log2(np.mean(s**2)) / 2))
    return {"x": bf(np.random.standard_normal((B, S, D)) * 0.5 * s * p),
            "weight": bf(np.random.standard_normal((F, D)) * 0.5 / s * q),
            "alpha": bf(1.0 + 0.1 * np.random.standard_normal(1)),
            "bias": bf(0.1 * np.random.standard_normal(F))}


def reference(x, weight, alpha, bias):
    x = f64(x)
    weight = f64(weight)
    nf = weight.shape[0]
    y = mxq(x, 2, "e4m3") @ mxq(weight, 1, "e4m3").T
    x_sq = np.sum(x * x, axis=-1, keepdims=True)
    w_sq = np.sum(weight * weight, axis=-1)
    distances = x_sq + w_sq - 2.0 * y
    out = (y * y) / (distances + EPS)
    scale = (np.sqrt(nf) / np.log(1.0 + nf)) ** f64(alpha)
    out = out * scale + f64(bias)
    return out

@@ -1,0 +1,170 @@
+import math
+from contextlib import ExitStack
+
+import concourse.mybir as mybir
+from concourse.masks import make_identity
+
+F32 = mybir.dt.float32
+BF16 = mybir.dt.bfloat16
+U32 = mybir.dt.uint32
+U8 = mybir.dt.uint8
+FP8X4 = mybir.dt.float8_e4m3fn_x4
+ALU = mybir.AluOpType
+ACT = mybir.ActivationFunctionType
+
+P = 128
+PACK = 4
+TOKENS = 4096
+K = 512
+FEATS = 1024
+TOKEN_TILES = TOKENS // P
+FEAT_TILES = FEATS // P
+BANK = 512
+HALVES = FEATS // BANK
+GROUP = 8
+EPS = 1e-6
+ROOT_OF_BASE = math.sqrt(math.sqrt(FEATS) / math.log(1.0 + FEATS))
+
+FLOPS = 2 * TOKENS * K * FEATS
+
+
+def pack_for_mx(nc, psum_t, stage, ident, words, first, codes, scales):
+    grouped = stage.tile([P, GROUP * P * PACK], BF16, align_bytes=64)
+    grouped_words = grouped[:].bitcast(F32).rearrange("p (j r u) -> p j r u", r=P, u=2)
+    for pair in range(GROUP // 2):
+        turned = psum_t.tile([P, 2, 2, P], F32, tag="turned")
+        for jj in range(2):
+            for u in range(2):
+                nc.tensor.transpose(
+                    turned[:, jj, u, :],
+                    words[:, (first + 2 * pair + jj) * (K // 2) + u * P : (first + 2 * pair + jj) * (K // 2) + (u + 1) * P],
+                    ident[:],
+                )
+        nc.vector.tensor_copy(
+            out=grouped_words[:, 2 * pair : 2 * pair + 2, :, :],
+            in_=turned[:].rearrange("p j u r -> p j r u"),
+        )
+    cols = slice(first * P, (first + GROUP) * P)
+    nc.vector.quantize_mx(
+        out=codes[:, cols].bitcast(FP8X4),
+        scales=scales[:, cols],
+        in_=grouped[:],
+    )
+
+
+def tile_yatdense_t_kernel(tc, x, weight, alpha, bias, out):
+    nc = tc.nc
+    x_view = x.flatten_outer_dims().rearrange("(p j) k -> p (j k)", j=TOKEN_TILES)
+    out_view = out.flatten_outer_dims().rearrange("(p j) n -> p j n", j=TOKEN_TILES)
+    w_view = weight.rearrange("(i p) k -> p i k", p=P)
+
+    with ExitStack() as ctx:
+        keep = ctx.enter_context(tc.tile_pool(name="keep", bufs=1))
+        stage = ctx.enter_context(tc.tile_pool(name="stage", bufs=2))
+        work = ctx.enter_context(tc.tile_pool(name="work", bufs=3))
+        psum_t = ctx.enter_context(tc.psum_pool(name="psum_t", bufs=2))
+        psum_y = ctx.enter_context(tc.psum_pool(name="psum_y", bufs=6))
+
+        w_sb = keep.tile([P, FEAT_TILES * K], BF16)
+        x_sb = keep.tile([P, TOKEN_TILES * K], BF16)
+        alpha_bf = keep.tile([P, 1], BF16)
+        bias_bf = keep.tile([P, FEATS], BF16)
+        nc.sync.dma_start(out=w_sb[:, 0 : 4 * K].rearrange("p (i k) -> p i k", k=K), in_=w_view[:, 0:4, :])
+        nc.sync.dma_start(out=w_sb[:, 4 * K : 8 * K].rearrange("p (i k) -> p i k", k=K), in_=w_view[:, 4:8, :])
+        nc.sync.dma_start(out=x_sb[:, 0 : GROUP * K], in_=x_view[:, 0 : GROUP * K])
+        nc.sync.dma_start(out=alpha_bf[:], in_=alpha.partition_broadcast(P))
+        nc.sync.dma_start(out=bias_bf[:], in_=bias.partition_broadcast(P))
+        for g in range(1, TOKEN_TILES // GROUP):
+            nc.sync.dma_start(
+                out=x_sb[:, g * GROUP * K : (g + 1) * GROUP * K],
+                in_=x_view[:, g * GROUP * K : (g + 1) * GROUP * K],
+            )
+
+        ident = keep.tile([P, P], F32)
+        make_identity(nc, ident[:])
+
+        alpha_f = keep.tile([P, 1], F32)
+        nc.gpsimd.tensor_copy(out=alpha_f[:], in_=alpha_bf[:])
+        root = keep.tile([P, 1], F32)
+        nc.gpsimd.tensor_scalar(
+            out=root[:], in0=alpha_f[:], scalar1=0.0, scalar2=ROOT_OF_BASE, op0=ALU.mult, op1=ALU.add
+        )
+        sigma = keep.tile([P, 1], F32)
+        nc.gpsimd.tensor_tensor(out=sigma[:], in0=root[:], in1=alpha_f[:], op=ALU.pow)
+
+        bias_rows = keep.tile([P, FEATS], F32)
+        nc.gpsimd.tensor_scalar(
+            out=bias_rows[:], in0=bias_bf[:], scalar1=1.0, scalar2=0.0, op0=ALU.mult, op1=ALU.add
+        )
+
+        w_codes = keep.tile([P, FEATS], U32, align_bytes=64)
+        w_scales = keep.tile([P, FEATS], U8, align_bytes=64)
+        pack_for_mx(nc, psum_t, stage, ident, w_sb[:].bitcast(F32), 0, w_codes, w_scales)
+
+        w_sq = keep.tile([P, FEAT_TILES], F32)
+        for i in range(FEAT_TILES):
+            squares = stage.tile([P, K], BF16, tag="squares")
+            nc.scalar.activation(
+                out=squares[:], in_=w_sb[:, i * K : (i + 1) * K], func=ACT.Square, accum_out=w_sq[:, i : i + 1]
+            )
+        spread = keep.tile([P, FEAT_TILES, P], F32)
+        nc.vector.tensor_copy(out=spread[:], in_=w_sq[:].unsqueeze(2).to_broadcast([P, FEAT_TILES, P]))
+        w_sq_rows = keep.tile([P, FEATS], F32)
+        for h in range(HALVES):
+            turned_sq = psum_t.tile([P, 4, P], F32, tag="turned")
+            for i in range(4):
+                nc.tensor.transpose(turned_sq[:, i, :], spread[:, 4 * h + i, :], ident[:])
+            nc.vector.tensor_scalar_add(
+                out=w_sq_rows[:, h * BANK : (h + 1) * BANK],
+                in0=turned_sq[:].rearrange("p i r -> p (i r)"),
+                scalar1=EPS,
+            )
+
+        x_codes = keep.tile([P, TOKENS], U32, align_bytes=64)
+        x_scales = keep.tile([P, TOKENS], U8, align_bytes=64)
+        x_sq = keep.tile([P, TOKEN_TILES], F32)
+        x_words = x_sb[:].bitcast(F32)
+
+        for g in range(TOKEN_TILES // GROUP):
+            pack_for_mx(nc, psum_t, stage, ident, x_words, g * GROUP, x_codes, x_scales)
+            for j in range(g * GROUP, (g + 1) * GROUP):
+                squares = stage.tile([P, K], BF16, tag="squares")
+                nc.scalar.activation(
+                    out=squares[:], in_=x_sb[:, j * K : (j + 1) * K], func=ACT.Square, accum_out=x_sq[:, j : j + 1]
+                )
+            for j in range(g * GROUP, (g + 1) * GROUP):
+                rows = slice(j * P, (j + 1) * P)
+                products = []
+                e = work.tile([P, FEATS], F32)
+                for h in range(HALVES):
+                    cols = slice(h * BANK, (h + 1) * BANK)
+                    y = psum_y.tile([P, BANK], F32)
+                    nc.tensor.matmul_mx(
+                        out=y[:],
+                        lhsT=x_codes[:, rows].bitcast(FP8X4),
+                        lhsT_scale=x_scales[:, rows],
+                        rhs=w_codes[:, cols].bitcast(FP8X4),
+                        rhs_scale=w_scales[:, cols],
+                        start=True,
+                        stop=True,
+                    )
+                    products.append(y)
+                    nc.vector.scalar_tensor_tensor(
+                        out=e[:, cols], in0=y[:], scalar=-2.0, in1=w_sq_rows[:, cols], op0=ALU.mult, op1=ALU.add
+                    )
+                q = work.tile([P, FEATS], F32)
+                nc.scalar.activation(
+                    out=q[:], in_=e[:], func=ACT.Abs_reciprocal_sqrt, bias=x_sq[:, j : j + 1], scale=1.0
+                )
+                t = work.tile([P, FEATS], F32)
+                for h in range(HALVES):
+                    cols = slice(h * BANK, (h + 1) * BANK)
+                    nc.vector.scalar_tensor_tensor(
+                        out=t[:, cols], in0=products[h][:], scalar=sigma[:, 0:1], in1=q[:, cols],
+                        op0=ALU.mult, op1=ALU.mult,
+                    )
+                sq = work.tile([P, FEATS], F32)
+                nc.scalar.activation(out=sq[:], in_=t[:], func=ACT.Square)
+                o = work.tile([P, FEATS], F32)
+                nc.gpsimd.tensor_tensor(out=o[:], in0=sq[:], in1=bias_rows[:], op=ALU.add)
+                nc.sync.dma_start(out=out_view[:, j, :], in_=o[:])

@@ -21,35 +21,16 @@ TOKEN_TILES = TOKENS // P
 FEAT_TILES = FEATS // P
 BANK = 512
 HALVES = FEATS // BANK
-GROUP = 8
+GROUP = 4
 EPS = 1e-6
 ROOT_OF_BASE = math.sqrt(math.sqrt(FEATS) / math.log(1.0 + FEATS))
+VECTOR_TAIL = 2
 
 FLOPS = 2 * TOKENS * K * FEATS
 
-
-def pack_for_mx(nc, psum_t, stage, ident, words, first, codes, scales):
-    grouped = stage.tile([P, GROUP * P * PACK], BF16, align_bytes=64)
-    grouped_words = grouped[:].bitcast(F32).rearrange("p (j r u) -> p j r u", r=P, u=2)
-    for pair in range(GROUP // 2):
-        turned = psum_t.tile([P, 2, 2, P], F32, tag="turned")
-        for jj in range(2):
-            for u in range(2):
-                nc.tensor.transpose(
-                    turned[:, jj, u, :],
-                    words[:, (first + 2 * pair + jj) * (K // 2) + u * P : (first + 2 * pair + jj) * (K // 2) + (u + 1) * P],
-                    ident[:],
-                )
-        nc.vector.tensor_copy(
-            out=grouped_words[:, 2 * pair : 2 * pair + 2, :, :],
-            in_=turned[:].rearrange("p j u r -> p j r u"),
-        )
-    cols = slice(first * P, (first + GROUP) * P)
-    nc.vector.quantize_mx(
-        out=codes[:, cols].bitcast(FP8X4),
-        scales=scales[:, cols],
-        in_=grouped[:],
-    )
+COPY_STEP = {4: -2, 5: -1, 6: 0, 7: 1, 8: 3, 9: 5, 10: 7, 11: 9, 12: 11, 13: 13, 14: 15, 15: 17}
+SQUARE_STEP = {-2: [6, 7], -1: [8, 9], 0: [10, 11], 1: [12]}
+BIAS_BANK_STEP = 19
 
 
 def tile_yatdense_t_kernel(tc, x, weight, alpha, bias, out):
@@ -60,28 +41,100 @@ def tile_yatdense_t_kernel(tc, x, weight, alpha, bias, out):
 
     with ExitStack() as ctx:
         keep = ctx.enter_context(tc.tile_pool(name="keep", bufs=1))
-        stage = ctx.enter_context(tc.tile_pool(name="stage", bufs=2))
+        stage = ctx.enter_context(tc.tile_pool(name="stage", bufs=3))
         work = ctx.enter_context(tc.tile_pool(name="work", bufs=3))
-        psum_t = ctx.enter_context(tc.psum_pool(name="psum_t", bufs=2))
-        psum_y = ctx.enter_context(tc.psum_pool(name="psum_y", bufs=6))
+        store = ctx.enter_context(tc.tile_pool(name="store", bufs=4))
+        psum = ctx.enter_context(tc.psum_pool(name="psum", bufs=1))
+        ctx.enter_context(tc.manual_schedule())
+
+        def bank(n):
+            return psum.tile([P, BANK], F32, name="bank%d" % n)
 
         w_sb = keep.tile([P, FEAT_TILES * K], BF16)
         x_sb = keep.tile([P, TOKEN_TILES * K], BF16)
         alpha_bf = keep.tile([P, 1], BF16)
         bias_bf = keep.tile([P, FEATS], BF16)
+
+        def load_x(first, last):
+            nc.sync.dma_start(out=x_sb[:, first * K : last * K], in_=x_view[:, first * K : last * K])
+
         nc.sync.dma_start(out=w_sb[:, 0 : 4 * K].rearrange("p (i k) -> p i k", k=K), in_=w_view[:, 0:4, :])
         nc.sync.dma_start(out=w_sb[:, 4 * K : 8 * K].rearrange("p (i k) -> p i k", k=K), in_=w_view[:, 4:8, :])
-        nc.sync.dma_start(out=x_sb[:, 0 : GROUP * K], in_=x_view[:, 0 : GROUP * K])
+        load_x(0, 4)
         nc.sync.dma_start(out=alpha_bf[:], in_=alpha.partition_broadcast(P))
+        load_x(4, 8)
+        load_x(8, 16)
         nc.sync.dma_start(out=bias_bf[:], in_=bias.partition_broadcast(P))
-        for g in range(1, TOKEN_TILES // GROUP):
-            nc.sync.dma_start(
-                out=x_sb[:, g * GROUP * K : (g + 1) * GROUP * K],
-                in_=x_view[:, g * GROUP * K : (g + 1) * GROUP * K],
-            )
+        load_x(16, 24)
+        load_x(24, 32)
 
         ident = keep.tile([P, P], F32)
         make_identity(nc, ident[:])
+        ident_bf = keep.tile([P, P], BF16)
+        make_identity(nc, ident_bf[:])
+
+        one = keep.tile([P, 1], F32)
+        nc.vector.memset(one[:], 1.0)
+        warm = keep.tile([P, 1], F32)
+        nc.scalar.activation(out=warm[:], in_=one[:], func=ACT.Abs_reciprocal_sqrt)
+
+        w_codes = keep.tile([P, FEATS], U32, align_bytes=64)
+        w_scales = keep.tile([P, FEATS], U8, align_bytes=64)
+        x_codes = keep.tile([P, TOKENS], U32, align_bytes=64)
+        x_scales = keep.tile([P, TOKENS], U8, align_bytes=64)
+        w_sq = keep.tile([P, FEAT_TILES], F32)
+        x_sq = keep.tile([P, TOKEN_TILES], F32)
+        w_words = w_sb[:].bitcast(F32)
+        x_words = x_sb[:].bitcast(F32)
+
+        def turn(words, first, n):
+            turned = bank(n)
+            view = turned[:].rearrange("p (j u r) -> p j u r", j=2, u=2)
+            for jj in range(2):
+                for u in range(2):
+                    c0 = (first + jj) * (K // 2) + u * P
+                    nc.tensor.transpose(view[:, jj, u, :], words[:, c0 : c0 + P], ident[:])
+            return turned
+
+        def new_group():
+            return stage.tile([P, GROUP * P * PACK], BF16, name="grouped", align_bytes=64)
+
+        def regroup(turned, grouped, half):
+            dst = grouped[:].bitcast(F32).rearrange("p (j r u) -> p j r u", r=P, u=2)
+            nc.vector.tensor_copy(
+                out=dst[:, 2 * half : 2 * half + 2, :, :],
+                in_=turned[:].rearrange("p (j u r) -> p j r u", j=2, u=2),
+            )
+
+        def quantise(grouped, codes, scales, group):
+            cols = slice(group * GROUP * P, (group + 1) * GROUP * P)
+            nc.vector.quantize_mx(out=codes[:, cols].bitcast(FP8X4), scales=scales[:, cols], in_=grouped[:])
+
+        def square_sum(src, j, dst):
+            junk = stage.tile([P, K], BF16, name="junk")
+            nc.scalar.activation(out=junk[:], in_=src[:, j * K : (j + 1) * K], func=ACT.Square, accum_out=dst[:, j : j + 1])
+
+        tw = [turn(w_words, 2 * m, m) for m in range(4)]
+        for i in range(FEAT_TILES):
+            square_sum(w_sb, i, w_sq)
+        gw0 = new_group()
+        gw1 = new_group()
+        regroup(tw[0], gw0, 0)
+        regroup(tw[1], gw0, 1)
+        regroup(tw[2], gw1, 0)
+        quantise(gw0, w_codes, w_scales, 0)
+        regroup(tw[3], gw1, 1)
+        tx = [turn(x_words, 2 * m, 4 + m) for m in range(4)]
+        gx0 = new_group()
+        regroup(tx[0], gx0, 0)
+        quantise(gw1, w_codes, w_scales, 1)
+        regroup(tx[1], gx0, 1)
+        gx1 = new_group()
+        regroup(tx[2], gx1, 0)
+        quantise(gx0, x_codes, x_scales, 0)
+        regroup(tx[3], gx1, 1)
+        for j in range(6):
+            square_sum(x_sb, j, x_sq)
 
         alpha_f = keep.tile([P, 1], F32)
         nc.gpsimd.tensor_copy(out=alpha_f[:], in_=alpha_bf[:])
@@ -91,80 +144,110 @@ def tile_yatdense_t_kernel(tc, x, weight, alpha, bias, out):
         )
         sigma = keep.tile([P, 1], F32)
         nc.gpsimd.tensor_tensor(out=sigma[:], in0=root[:], in1=alpha_f[:], op=ALU.pow)
-
         bias_rows = keep.tile([P, FEATS], F32)
         nc.gpsimd.tensor_scalar(
             out=bias_rows[:], in0=bias_bf[:], scalar1=1.0, scalar2=0.0, op0=ALU.mult, op1=ALU.add
         )
 
-        w_codes = keep.tile([P, FEATS], U32, align_bytes=64)
-        w_scales = keep.tile([P, FEATS], U8, align_bytes=64)
-        pack_for_mx(nc, psum_t, stage, ident, w_sb[:].bitcast(F32), 0, w_codes, w_scales)
+        y = {}
+        e = {}
+        q = {}
+        t = {}
+        sq = {}
+        halves = [slice(h * BANK, (h + 1) * BANK) for h in range(HALVES)]
 
-        w_sq = keep.tile([P, FEAT_TILES], F32)
-        for i in range(FEAT_TILES):
-            squares = stage.tile([P, K], BF16, tag="squares")
-            nc.scalar.activation(
-                out=squares[:], in_=w_sb[:, i * K : (i + 1) * K], func=ACT.Square, accum_out=w_sq[:, i : i + 1]
-            )
-        spread = keep.tile([P, FEAT_TILES, P], F32)
-        nc.vector.tensor_copy(out=spread[:], in_=w_sq[:].unsqueeze(2).to_broadcast([P, FEAT_TILES, P]))
+        def multiply(k):
+            rows = slice(k * P, (k + 1) * P)
+            y[k] = []
+            for h in range(HALVES):
+                product = bank((2 + 2 * k) % 6 + h)
+                nc.tensor.matmul_mx(
+                    out=product[:],
+                    lhsT=x_codes[:, rows].bitcast(FP8X4),
+                    lhsT_scale=x_scales[:, rows],
+                    rhs=w_codes[:, halves[h]].bitcast(FP8X4),
+                    rhs_scale=w_scales[:, halves[h]],
+                    start=True,
+                    stop=True,
+                )
+                y[k].append(product)
+
+        multiply(0)
+        multiply(1)
+
         w_sq_rows = keep.tile([P, FEATS], F32)
+        spread = [bank(0), bank(1)]
+        for i in range(FEAT_TILES):
+            nc.tensor.transpose(
+                spread[i // 4][:, (i % 4) * P : (i % 4 + 1) * P], w_sq[:, i : i + 1].to_broadcast([P, P]), ident[:]
+            )
+        turned = {4: turn(x_words, 8, 6)}
+        quantise(gx1, x_codes, x_scales, 1)
         for h in range(HALVES):
-            turned_sq = psum_t.tile([P, 4, P], F32, tag="turned")
-            for i in range(4):
-                nc.tensor.transpose(turned_sq[:, i, :], spread[:, 4 * h + i, :], ident[:])
-            nc.vector.tensor_scalar_add(
-                out=w_sq_rows[:, h * BANK : (h + 1) * BANK],
-                in0=turned_sq[:].rearrange("p i r -> p (i r)"),
-                scalar1=EPS,
+            nc.vector.tensor_scalar_add(out=w_sq_rows[:, halves[h]], in0=spread[h][:], scalar1=EPS)
+
+        def stage_a(k):
+            e[k] = work.tile([P, FEATS], F32, name="e")
+            for h in range(HALVES):
+                nc.vector.scalar_tensor_tensor(
+                    out=e[k][:, halves[h]], in0=y[k][h][:], scalar=-2.0, in1=w_sq_rows[:, halves[h]],
+                    op0=ALU.mult, op1=ALU.add,
+                )
+
+        def stage_b(k):
+            q[k] = work.tile([P, FEATS], F32, name="q")
+            nc.scalar.activation(
+                out=q[k][:], in_=e[k][:], func=ACT.Abs_reciprocal_sqrt, bias=x_sq[:, k : k + 1], scale=1.0
             )
 
-        x_codes = keep.tile([P, TOKENS], U32, align_bytes=64)
-        x_scales = keep.tile([P, TOKENS], U8, align_bytes=64)
-        x_sq = keep.tile([P, TOKEN_TILES], F32)
-        x_words = x_sb[:].bitcast(F32)
+        def stage_c(k):
+            t[k] = work.tile([P, FEATS], F32, name="t")
+            for h in range(HALVES):
+                nc.vector.tensor_tensor(out=t[k][:, halves[h]], in0=y[k][h][:], in1=q[k][:, halves[h]], op=ALU.mult)
 
-        for g in range(TOKEN_TILES // GROUP):
-            pack_for_mx(nc, psum_t, stage, ident, x_words, g * GROUP, x_codes, x_scales)
-            for j in range(g * GROUP, (g + 1) * GROUP):
-                squares = stage.tile([P, K], BF16, tag="squares")
-                nc.scalar.activation(
-                    out=squares[:], in_=x_sb[:, j * K : (j + 1) * K], func=ACT.Square, accum_out=x_sq[:, j : j + 1]
-                )
-            for j in range(g * GROUP, (g + 1) * GROUP):
-                rows = slice(j * P, (j + 1) * P)
-                products = []
-                e = work.tile([P, FEATS], F32)
+        def stage_d(k):
+            sq[k] = work.tile([P, FEATS], F32, name="sq")
+            nc.scalar.activation(out=sq[k][:], in_=t[k][:], func=ACT.Square, scale=sigma[:, 0:1])
+
+        bias_bank = []
+
+        def stage_e(k):
+            o = store.tile([P, FEATS], F32, name="o")
+            if k < TOKEN_TILES - VECTOR_TAIL:
+                nc.gpsimd.tensor_tensor(out=o[:], in0=sq[k][:], in1=bias_rows[:], op=ALU.add)
+                nc.sync.dma_start(out=out_view[:, k, :], in_=o[:])
+            else:
                 for h in range(HALVES):
-                    cols = slice(h * BANK, (h + 1) * BANK)
-                    y = psum_y.tile([P, BANK], F32)
-                    nc.tensor.matmul_mx(
-                        out=y[:],
-                        lhsT=x_codes[:, rows].bitcast(FP8X4),
-                        lhsT_scale=x_scales[:, rows],
-                        rhs=w_codes[:, cols].bitcast(FP8X4),
-                        rhs_scale=w_scales[:, cols],
-                        start=True,
-                        stop=True,
-                    )
-                    products.append(y)
-                    nc.vector.scalar_tensor_tensor(
-                        out=e[:, cols], in0=y[:], scalar=-2.0, in1=w_sq_rows[:, cols], op0=ALU.mult, op1=ALU.add
-                    )
-                q = work.tile([P, FEATS], F32)
-                nc.scalar.activation(
-                    out=q[:], in_=e[:], func=ACT.Abs_reciprocal_sqrt, bias=x_sq[:, j : j + 1], scale=1.0
-                )
-                t = work.tile([P, FEATS], F32)
+                    nc.vector.tensor_tensor(out=o[:, halves[h]], in0=sq[k][:, halves[h]], in1=bias_bank[h][:], op=ALU.add)
+                    nc.sync.dma_start(out=out_view[:, k, halves[h]], in_=o[:, halves[h]])
+
+        groups = {}
+        for i in range(-2, TOKEN_TILES + 2):
+            if 2 <= i + 2 < TOKEN_TILES:
+                multiply(i + 2)
+            for m in range(5, 16):
+                if COPY_STEP[m] == i + 1:
+                    turned[m] = turn(x_words, 2 * m, 6 + m % 2)
+            if i == BIAS_BANK_STEP:
                 for h in range(HALVES):
-                    cols = slice(h * BANK, (h + 1) * BANK)
-                    nc.vector.scalar_tensor_tensor(
-                        out=t[:, cols], in0=products[h][:], scalar=sigma[:, 0:1], in1=q[:, cols],
-                        op0=ALU.mult, op1=ALU.mult,
-                    )
-                sq = work.tile([P, FEATS], F32)
-                nc.scalar.activation(out=sq[:], in_=t[:], func=ACT.Square)
-                o = work.tile([P, FEATS], F32)
-                nc.gpsimd.tensor_tensor(out=o[:], in0=sq[:], in1=bias_rows[:], op=ALU.add)
-                nc.sync.dma_start(out=out_view[:, j, :], in_=o[:])
+                    bias_bank.append(bank(6 + h))
+                    nc.tensor.matmul(out=bias_bank[h][:], lhsT=ident_bf[:], rhs=bias_bf[:, halves[h]], start=True, stop=True)
+            for m in range(4, 16):
+                if m % 2 == 1 and COPY_STEP[m] == i - 1:
+                    quantise(groups[m // 2], x_codes, x_scales, m // 2)
+                if COPY_STEP[m] == i:
+                    if m % 2 == 0:
+                        groups[m // 2] = new_group()
+                    regroup(turned[m], groups[m // 2], m % 2)
+            if 0 <= i < TOKEN_TILES:
+                stage_c(i)
+            if 0 <= i + 2 < TOKEN_TILES:
+                stage_a(i + 2)
+            if 0 <= i - 1 < TOKEN_TILES:
+                stage_d(i - 1)
+            if 0 <= i + 1 < TOKEN_TILES:
+                stage_b(i + 1)
+            for j in SQUARE_STEP.get(i, [i + 11] if 2 <= i and i + 11 < TOKEN_TILES else []):
+                square_sum(x_sb, j, x_sq)
+            if 0 <= i - 2 < TOKEN_TILES:
+                stage_e(i - 2)

@@ -28,9 +28,15 @@ VECTOR_TAIL = 2
 
 FLOPS = 2 * TOKENS * K * FEATS
 
-COPY_STEP = {4: -2, 5: -1, 6: 0, 7: 1, 8: 3, 9: 5, 10: 7, 11: 9, 12: 11, 13: 13, 14: 15, 15: 17}
-SQUARE_STEP = {-2: [6, 7], -1: [8, 9], 0: [10, 11], 1: [12]}
-BIAS_BANK_STEP = 19
+PAIRS = TOKEN_TILES // 2
+HEAD_PAIRS = 4
+GRAM_FIRST = 5
+SQUARE_STEP = {-2: [6, 7], -1: [8, 9]}
+BIAS_BANK_STEP = 23
+
+
+def turn_step(m):
+    return 2 * m - 11
 
 
 def tile_yatdense_t_kernel(tc, x, weight, alpha, bias, out):
@@ -58,8 +64,10 @@ def tile_yatdense_t_kernel(tc, x, weight, alpha, bias, out):
         def load_x(first, last):
             nc.sync.dma_start(out=x_sb[:, first * K : last * K], in_=x_view[:, first * K : last * K])
 
-        nc.sync.dma_start(out=w_sb[:, 0 : 4 * K].rearrange("p (i k) -> p i k", k=K), in_=w_view[:, 0:4, :])
-        nc.sync.dma_start(out=w_sb[:, 4 * K : 8 * K].rearrange("p (i k) -> p i k", k=K), in_=w_view[:, 4:8, :])
+        for first, last in ((0, 2), (2, 4), (4, 8)):
+            nc.sync.dma_start(
+                out=w_sb[:, first * K : last * K].rearrange("p (i k) -> p i k", k=K), in_=w_view[:, first:last, :]
+            )
         load_x(0, 4)
         nc.sync.dma_start(out=alpha_bf[:], in_=alpha.partition_broadcast(P))
         load_x(4, 8)
@@ -84,6 +92,7 @@ def tile_yatdense_t_kernel(tc, x, weight, alpha, bias, out):
         x_scales = keep.tile([P, TOKENS], U8, align_bytes=64)
         w_sq = keep.tile([P, FEAT_TILES], F32)
         x_sq = keep.tile([P, TOKEN_TILES], F32)
+        x_sq_gram = keep.tile([P, TOKEN_TILES], F32)
         w_words = w_sb[:].bitcast(F32)
         x_words = x_sb[:].bitcast(F32)
 
@@ -99,12 +108,13 @@ def tile_yatdense_t_kernel(tc, x, weight, alpha, bias, out):
         def new_group():
             return stage.tile([P, GROUP * P * PACK], BF16, name="grouped", align_bytes=64)
 
-        def regroup(turned, grouped, half):
-            dst = grouped[:].bitcast(F32).rearrange("p (j r u) -> p j r u", r=P, u=2)
-            nc.vector.tensor_copy(
-                out=dst[:, 2 * half : 2 * half + 2, :, :],
-                in_=turned[:].rearrange("p (j u r) -> p j r u", j=2, u=2),
-            )
+        def regroup(turned, grouped, half, on_scalar=False):
+            dst = grouped[:].bitcast(F32).rearrange("p (j r u) -> p j r u", r=P, u=2)[:, 2 * half : 2 * half + 2, :, :]
+            src = turned[:].rearrange("p (j u r) -> p j r u", j=2, u=2)
+            if on_scalar:
+                nc.scalar.copy(out=dst, in_=src)
+            else:
+                nc.vector.tensor_copy(out=dst, in_=src)
 
         def quantise(grouped, codes, scales, group):
             cols = slice(group * GROUP * P, (group + 1) * GROUP * P)
@@ -181,7 +191,6 @@ def tile_yatdense_t_kernel(tc, x, weight, alpha, bias, out):
             nc.tensor.transpose(
                 spread[i // 4][:, (i % 4) * P : (i % 4 + 1) * P], w_sq[:, i : i + 1].to_broadcast([P, P]), ident[:]
             )
-        turned = {4: turn(x_words, 8, 6)}
         quantise(gx1, x_codes, x_scales, 1)
         for h in range(HALVES):
             nc.vector.tensor_scalar_add(out=w_sq_rows[:, halves[h]], in0=spread[h][:], scalar1=EPS)
@@ -197,7 +206,7 @@ def tile_yatdense_t_kernel(tc, x, weight, alpha, bias, out):
         def stage_b(k):
             q[k] = work.tile([P, FEATS], F32, name="q")
             nc.scalar.activation(
-                out=q[k][:], in_=e[k][:], func=ACT.Abs_reciprocal_sqrt, bias=x_sq[:, k : k + 1], scale=1.0
+                out=q[k][:], in_=e[k][:], func=ACT.Abs_reciprocal_sqrt, bias=(x_sq if k < 2 * GRAM_FIRST else x_sq_gram)[:, k : k + 1], scale=1.0
             )
 
         def stage_c(k):
@@ -221,24 +230,46 @@ def tile_yatdense_t_kernel(tc, x, weight, alpha, bias, out):
                     nc.vector.tensor_tensor(out=o[:, halves[h]], in0=sq[k][:, halves[h]], in1=bias_bank[h][:], op=ALU.add)
                     nc.sync.dma_start(out=out_view[:, k, halves[h]], in_=o[:, halves[h]])
 
+        turned = {}
         groups = {}
-        for i in range(-2, TOKEN_TILES + 2):
+        gram = {}
+
+        def gram_products(m):
+            gram[m] = bank(7)
+            view = groups[m // 2][:].rearrange("p (j r t) -> p j r t", r=P, t=PACK)
+            for jj in range(2):
+                for tt in range(PACK):
+                    operand = view[:, 2 * (m % 2) + jj, :, tt]
+                    nc.tensor.matmul(
+                        out=gram[m][:, jj * P : (jj + 1) * P], lhsT=operand, rhs=operand,
+                        start=(tt == 0), stop=(tt == PACK - 1),
+                    )
+
+        def gram_diagonals(m):
+            for jj in range(2):
+                masked = stage.tile([P, P], F32, name="masked")
+                nc.vector.scalar_tensor_tensor(
+                    out=masked[:], in0=gram[m][:, jj * P : (jj + 1) * P], scalar=1.0, in1=ident[:],
+                    op0=ALU.mult, op1=ALU.mult, accum_out=x_sq_gram[:, 2 * m + jj : 2 * m + jj + 1],
+                )
+
+        for i in range(-3, TOKEN_TILES + 2):
             if 2 <= i + 2 < TOKEN_TILES:
                 multiply(i + 2)
-            for m in range(5, 16):
-                if COPY_STEP[m] == i + 1:
-                    turned[m] = turn(x_words, 2 * m, 6 + m % 2)
+            for m in range(HEAD_PAIRS, PAIRS):
+                if m >= GRAM_FIRST and turn_step(m) + 2 == i:
+                    gram_products(m)
+                if turn_step(m) == i:
+                    turned[m] = turn(x_words, 2 * m, 6)
             if i == BIAS_BANK_STEP:
                 for h in range(HALVES):
                     bias_bank.append(bank(6 + h))
                     nc.tensor.matmul(out=bias_bank[h][:], lhsT=ident_bf[:], rhs=bias_bf[:, halves[h]], start=True, stop=True)
-            for m in range(4, 16):
-                if m % 2 == 1 and COPY_STEP[m] == i - 1:
+            for m in range(HEAD_PAIRS, PAIRS):
+                if m % 2 == 1 and turn_step(m) + 2 == i:
                     quantise(groups[m // 2], x_codes, x_scales, m // 2)
-                if COPY_STEP[m] == i:
-                    if m % 2 == 0:
-                        groups[m // 2] = new_group()
-                    regroup(turned[m], groups[m // 2], m % 2)
+                if m >= GRAM_FIRST and turn_step(m) + 3 == i:
+                    gram_diagonals(m)
             if 0 <= i < TOKEN_TILES:
                 stage_c(i)
             if 0 <= i + 2 < TOKEN_TILES:
@@ -247,7 +278,12 @@ def tile_yatdense_t_kernel(tc, x, weight, alpha, bias, out):
                 stage_d(i - 1)
             if 0 <= i + 1 < TOKEN_TILES:
                 stage_b(i + 1)
-            for j in SQUARE_STEP.get(i, [i + 11] if 2 <= i and i + 11 < TOKEN_TILES else []):
+            for m in range(HEAD_PAIRS, PAIRS):
+                if turn_step(m) + 1 == i:
+                    if m % 2 == 0:
+                        groups[m // 2] = new_group()
+                    regroup(turned[m], groups[m // 2], m % 2, on_scalar=True)
+            for j in SQUARE_STEP.get(i, []):
                 square_sum(x_sb, j, x_sq)
             if 0 <= i - 2 < TOKEN_TILES:
                 stage_e(i - 2)

@@ -19,24 +19,44 @@ K = 512
 FEATS = 1024
 TOKEN_TILES = TOKENS // P
 FEAT_TILES = FEATS // P
+PAIRS = TOKEN_TILES // 2
 BANK = 512
 HALVES = FEATS // BANK
 GROUP = 4
 EPS = 1e-6
 ROOT_OF_BASE = math.sqrt(math.sqrt(FEATS) / math.log(1.0 + FEATS))
-VECTOR_TAIL = 2
 
 FLOPS = 2 * TOKENS * K * FEATS
 
-PAIRS = TOKEN_TILES // 2
-HEAD_PAIRS = 4
-GRAM_FIRST = 5
-SQUARE_STEP = {-2: [6, 7], -1: [8, 9]}
-BIAS_BANK_STEP = 23
+FIRST_STEP = -2
+VECTOR_TAIL = 2
+GRAM_PAIRS = range(3, 14)
+VECTOR_COPIES = (12, 14)
+BIAS_BANK_STEP = 26
 
 
 def turn_step(m):
-    return 2 * m - 11
+    return m // 2 - 4
+
+
+def turn_bank(m):
+    return m - 2 if m < 6 else 4 + m % 2
+
+
+def quantise_step(g):
+    return g - 2
+
+
+def gram_step(m):
+    return max(m + 1, 2 * m - 4)
+
+
+def square_step(j):
+    return j - 3 if j < 6 else 2 * (j - 23)
+
+
+def product_bank(k, h):
+    return (6, 0, 2)[k % 3] + h
 
 
 def tile_yatdense_t_kernel(tc, x, weight, alpha, bias, out):
@@ -72,9 +92,9 @@ def tile_yatdense_t_kernel(tc, x, weight, alpha, bias, out):
         nc.sync.dma_start(out=alpha_bf[:], in_=alpha.partition_broadcast(P))
         load_x(4, 8)
         load_x(8, 16)
-        nc.sync.dma_start(out=bias_bf[:], in_=bias.partition_broadcast(P))
         load_x(16, 24)
         load_x(24, 32)
+        nc.sync.dma_start(out=bias_bf[:], in_=bias.partition_broadcast(P))
 
         ident = keep.tile([P, P], F32)
         make_identity(nc, ident[:])
@@ -86,6 +106,8 @@ def tile_yatdense_t_kernel(tc, x, weight, alpha, bias, out):
         warm = keep.tile([P, 1], F32)
         nc.scalar.activation(out=warm[:], in_=one[:], func=ACT.Abs_reciprocal_sqrt)
 
+        w_t = keep.tile([P, FEAT_TILES * K], BF16, align_bytes=64)
+        x_t = keep.tile([P, TOKEN_TILES * K], BF16, align_bytes=64)
         w_codes = keep.tile([P, FEATS], U32, align_bytes=64)
         w_scales = keep.tile([P, FEATS], U8, align_bytes=64)
         x_codes = keep.tile([P, TOKENS], U32, align_bytes=64)
@@ -93,84 +115,55 @@ def tile_yatdense_t_kernel(tc, x, weight, alpha, bias, out):
         w_sq = keep.tile([P, FEAT_TILES], F32)
         x_sq = keep.tile([P, TOKEN_TILES], F32)
         x_sq_gram = keep.tile([P, TOKEN_TILES], F32)
-        w_words = w_sb[:].bitcast(F32)
-        x_words = x_sb[:].bitcast(F32)
+        w_sq_rows = keep.tile([P, FEATS], F32)
+        sigma = keep.tile([P, 1], F32)
+        halves = [slice(h * BANK, (h + 1) * BANK) for h in range(HALVES)]
 
-        def turn(words, first, n):
-            turned = bank(n)
-            view = turned[:].rearrange("p (j u r) -> p j u r", j=2, u=2)
+        turned = {}
+
+        def turn(name, src, m, n):
+            turned[name, m] = bank(n)
+            view = turned[name, m][:].rearrange("p (j u r) -> p j u r", j=2, u=2)
+            words = src[:].bitcast(F32)
             for jj in range(2):
                 for u in range(2):
-                    c0 = (first + jj) * (K // 2) + u * P
+                    c0 = (2 * m + jj) * (K // 2) + u * P
                     nc.tensor.transpose(view[:, jj, u, :], words[:, c0 : c0 + P], ident[:])
-            return turned
 
-        def new_group():
-            return stage.tile([P, GROUP * P * PACK], BF16, name="grouped", align_bytes=64)
-
-        def regroup(turned, grouped, half, on_scalar=False):
-            dst = grouped[:].bitcast(F32).rearrange("p (j r u) -> p j r u", r=P, u=2)[:, 2 * half : 2 * half + 2, :, :]
-            src = turned[:].rearrange("p (j u r) -> p j r u", j=2, u=2)
+        def regroup(name, dst, m, on_scalar):
+            to = dst[:].bitcast(F32).rearrange("p (j r u) -> p j r u", r=P, u=2)[:, 2 * m : 2 * m + 2, :, :]
+            src = turned[name, m][:].rearrange("p (j u r) -> p j r u", j=2, u=2)
             if on_scalar:
-                nc.scalar.copy(out=dst, in_=src)
+                nc.scalar.copy(out=to, in_=src)
             else:
-                nc.vector.tensor_copy(out=dst, in_=src)
+                nc.vector.tensor_copy(out=to, in_=src)
 
-        def quantise(grouped, codes, scales, group):
-            cols = slice(group * GROUP * P, (group + 1) * GROUP * P)
-            nc.vector.quantize_mx(out=codes[:, cols].bitcast(FP8X4), scales=scales[:, cols], in_=grouped[:])
+        def quantise(src, codes, scales, g):
+            cols = slice(g * GROUP * P, (g + 1) * GROUP * P)
+            nc.vector.quantize_mx(
+                out=codes[:, cols].bitcast(FP8X4),
+                scales=scales[:, cols],
+                in_=src[:, g * GROUP * K : (g + 1) * GROUP * K],
+            )
 
         def square_sum(src, j, dst):
             junk = stage.tile([P, K], BF16, name="junk")
             nc.scalar.activation(out=junk[:], in_=src[:, j * K : (j + 1) * K], func=ACT.Square, accum_out=dst[:, j : j + 1])
-
-        tw = [turn(w_words, 2 * m, m) for m in range(4)]
-        for i in range(FEAT_TILES):
-            square_sum(w_sb, i, w_sq)
-        gw0 = new_group()
-        gw1 = new_group()
-        regroup(tw[0], gw0, 0)
-        regroup(tw[1], gw0, 1)
-        regroup(tw[2], gw1, 0)
-        quantise(gw0, w_codes, w_scales, 0)
-        regroup(tw[3], gw1, 1)
-        tx = [turn(x_words, 2 * m, 4 + m) for m in range(4)]
-        gx0 = new_group()
-        regroup(tx[0], gx0, 0)
-        quantise(gw1, w_codes, w_scales, 1)
-        regroup(tx[1], gx0, 1)
-        gx1 = new_group()
-        regroup(tx[2], gx1, 0)
-        quantise(gx0, x_codes, x_scales, 0)
-        regroup(tx[3], gx1, 1)
-        for j in range(6):
-            square_sum(x_sb, j, x_sq)
-
-        alpha_f = keep.tile([P, 1], F32)
-        nc.gpsimd.tensor_copy(out=alpha_f[:], in_=alpha_bf[:])
-        root = keep.tile([P, 1], F32)
-        nc.gpsimd.tensor_scalar(
-            out=root[:], in0=alpha_f[:], scalar1=0.0, scalar2=ROOT_OF_BASE, op0=ALU.mult, op1=ALU.add
-        )
-        sigma = keep.tile([P, 1], F32)
-        nc.gpsimd.tensor_tensor(out=sigma[:], in0=root[:], in1=alpha_f[:], op=ALU.pow)
-        bias_rows = keep.tile([P, FEATS], F32)
-        nc.gpsimd.tensor_scalar(
-            out=bias_rows[:], in0=bias_bf[:], scalar1=1.0, scalar2=0.0, op0=ALU.mult, op1=ALU.add
-        )
 
         y = {}
         e = {}
         q = {}
         t = {}
         sq = {}
-        halves = [slice(h * BANK, (h + 1) * BANK) for h in range(HALVES)]
+        o = {}
+        gram = {}
+        bias_bank = []
 
         def multiply(k):
             rows = slice(k * P, (k + 1) * P)
             y[k] = []
             for h in range(HALVES):
-                product = bank((2 + 2 * k) % 6 + h)
+                product = bank(product_bank(k, h))
                 nc.tensor.matmul_mx(
                     out=product[:],
                     lhsT=x_codes[:, rows].bitcast(FP8X4),
@@ -182,64 +175,12 @@ def tile_yatdense_t_kernel(tc, x, weight, alpha, bias, out):
                 )
                 y[k].append(product)
 
-        multiply(0)
-        multiply(1)
-
-        w_sq_rows = keep.tile([P, FEATS], F32)
-        spread = [bank(0), bank(1)]
-        for i in range(FEAT_TILES):
-            nc.tensor.transpose(
-                spread[i // 4][:, (i % 4) * P : (i % 4 + 1) * P], w_sq[:, i : i + 1].to_broadcast([P, P]), ident[:]
-            )
-        quantise(gx1, x_codes, x_scales, 1)
-        for h in range(HALVES):
-            nc.vector.tensor_scalar_add(out=w_sq_rows[:, halves[h]], in0=spread[h][:], scalar1=EPS)
-
-        def stage_a(k):
-            e[k] = work.tile([P, FEATS], F32, name="e")
-            for h in range(HALVES):
-                nc.vector.scalar_tensor_tensor(
-                    out=e[k][:, halves[h]], in0=y[k][h][:], scalar=-2.0, in1=w_sq_rows[:, halves[h]],
-                    op0=ALU.mult, op1=ALU.add,
-                )
-
-        def stage_b(k):
-            q[k] = work.tile([P, FEATS], F32, name="q")
-            nc.scalar.activation(
-                out=q[k][:], in_=e[k][:], func=ACT.Abs_reciprocal_sqrt, bias=(x_sq if k < 2 * GRAM_FIRST else x_sq_gram)[:, k : k + 1], scale=1.0
-            )
-
-        def stage_c(k):
-            t[k] = work.tile([P, FEATS], F32, name="t")
-            for h in range(HALVES):
-                nc.vector.tensor_tensor(out=t[k][:, halves[h]], in0=y[k][h][:], in1=q[k][:, halves[h]], op=ALU.mult)
-
-        def stage_d(k):
-            sq[k] = work.tile([P, FEATS], F32, name="sq")
-            nc.scalar.activation(out=sq[k][:], in_=t[k][:], func=ACT.Square, scale=sigma[:, 0:1])
-
-        bias_bank = []
-
-        def stage_e(k):
-            o = store.tile([P, FEATS], F32, name="o")
-            if k < TOKEN_TILES - VECTOR_TAIL:
-                nc.gpsimd.tensor_tensor(out=o[:], in0=sq[k][:], in1=bias_rows[:], op=ALU.add)
-                nc.sync.dma_start(out=out_view[:, k, :], in_=o[:])
-            else:
-                for h in range(HALVES):
-                    nc.vector.tensor_tensor(out=o[:, halves[h]], in0=sq[k][:, halves[h]], in1=bias_bank[h][:], op=ALU.add)
-                    nc.sync.dma_start(out=out_view[:, k, halves[h]], in_=o[:, halves[h]])
-
-        turned = {}
-        groups = {}
-        gram = {}
-
         def gram_products(m):
-            gram[m] = bank(7)
-            view = groups[m // 2][:].rearrange("p (j r t) -> p j r t", r=P, t=PACK)
+            gram[m] = bank(4 + m % 2)
+            view = x_t[:].rearrange("p (j r t) -> p j r t", r=P, t=PACK)
             for jj in range(2):
                 for tt in range(PACK):
-                    operand = view[:, 2 * (m % 2) + jj, :, tt]
+                    operand = view[:, 2 * m + jj, :, tt]
                     nc.tensor.matmul(
                         out=gram[m][:, jj * P : (jj + 1) * P], lhsT=operand, rhs=operand,
                         start=(tt == 0), stop=(tt == PACK - 1),
@@ -253,37 +194,128 @@ def tile_yatdense_t_kernel(tc, x, weight, alpha, bias, out):
                     op0=ALU.mult, op1=ALU.mult, accum_out=x_sq_gram[:, 2 * m + jj : 2 * m + jj + 1],
                 )
 
-        for i in range(-3, TOKEN_TILES + 2):
-            if 2 <= i + 2 < TOKEN_TILES:
+        def stage_a(k):
+            e[k] = work.tile([P, FEATS], F32, name="e")
+            for h in range(HALVES):
+                nc.vector.scalar_tensor_tensor(
+                    out=e[k][:, halves[h]], in0=y[k][h][:], scalar=-2.0, in1=w_sq_rows[:, halves[h]],
+                    op0=ALU.mult, op1=ALU.add,
+                )
+
+        def stage_b(k):
+            q[k] = work.tile([P, FEATS], F32, name="q")
+            nc.scalar.activation(
+                out=q[k][:], in_=e[k][:], func=ACT.Abs_reciprocal_sqrt,
+                bias=(x_sq_gram if k // 2 in GRAM_PAIRS else x_sq)[:, k : k + 1], scale=1.0,
+            )
+
+        def stage_c(k):
+            t[k] = work.tile([P, FEATS], F32, name="t")
+            for h in range(HALVES):
+                nc.vector.tensor_tensor(out=t[k][:, halves[h]], in0=y[k][h][:], in1=q[k][:, halves[h]], op=ALU.mult)
+
+        def stage_d(k):
+            sq[k] = work.tile([P, FEATS], F32, name="sq")
+            nc.scalar.activation(out=sq[k][:], in_=t[k][:], func=ACT.Square, scale=sigma[:, 0:1])
+
+        def stage_e(k):
+            o[k] = store.tile([P, FEATS], F32, name="o")
+            nc.gpsimd.tensor_tensor(out=o[k][:], in0=sq[k][:], in1=bias_bf[:], op=ALU.add)
+
+        def store_tile(k):
+            nc.sync.dma_start(out=out_view[:, k, :], in_=o[k][:])
+
+        def stage_e_vector(k):
+            o[k] = store.tile([P, FEATS], F32, name="o")
+            for h in range(HALVES):
+                nc.vector.tensor_tensor(out=o[k][:, halves[h]], in0=sq[k][:, halves[h]], in1=bias_bank[h][:], op=ALU.add)
+                nc.sync.dma_start(out=out_view[:, k, halves[h]], in_=o[k][:, halves[h]])
+
+        turn("w", w_sb, 0, 0)
+        turn("w", w_sb, 1, 1)
+        for i in range(4):
+            square_sum(w_sb, i, w_sq)
+        regroup("w", w_t, 0, False)
+        regroup("w", w_t, 1, False)
+        turn("w", w_sb, 2, 2)
+        turn("w", w_sb, 3, 3)
+        for i in range(4, FEAT_TILES):
+            square_sum(w_sb, i, w_sq)
+        quantise(w_t, w_codes, w_scales, 0)
+        regroup("w", w_t, 2, False)
+        regroup("w", w_t, 3, False)
+        turn("x", x_sb, 0, 4)
+        turn("x", x_sb, 1, 5)
+        regroup("x", x_t, 0, False)
+        quantise(w_t, w_codes, w_scales, 1)
+        regroup("x", x_t, 1, False)
+        turn("x", x_sb, 2, 6)
+        turn("x", x_sb, 3, 7)
+        spread = [bank(0), bank(1)]
+        for i in range(FEAT_TILES):
+            nc.tensor.transpose(
+                spread[i // 4][:, (i % 4) * P : (i % 4 + 1) * P], w_sq[:, i : i + 1].to_broadcast([P, P]), ident[:]
+            )
+        square_sum(x_sb, 0, x_sq)
+        regroup("x", x_t, 2, True)
+        regroup("x", x_t, 3, True)
+        quantise(x_t, x_codes, x_scales, 0)
+        for h in range(HALVES):
+            nc.vector.tensor_scalar_add(out=w_sq_rows[:, halves[h]], in0=spread[h][:], scalar1=EPS)
+
+        alpha_f = keep.tile([P, 1], F32)
+        nc.gpsimd.tensor_copy(out=alpha_f[:], in_=alpha_bf[:])
+        root = keep.tile([P, 1], F32)
+        nc.gpsimd.tensor_scalar(
+            out=root[:], in0=alpha_f[:], scalar1=0.0, scalar2=ROOT_OF_BASE, op0=ALU.mult, op1=ALU.add
+        )
+        nc.gpsimd.tensor_tensor(out=sigma[:], in0=root[:], in1=alpha_f[:], op=ALU.pow)
+
+        last = TOKEN_TILES - 1
+        for i in range(FIRST_STEP, last):
+            if i + 2 <= last:
                 multiply(i + 2)
-            for m in range(HEAD_PAIRS, PAIRS):
-                if m >= GRAM_FIRST and turn_step(m) + 2 == i:
-                    gram_products(m)
+            for m in range(4, PAIRS):
                 if turn_step(m) == i:
-                    turned[m] = turn(x_words, 2 * m, 6)
+                    turn("x", x_sb, m, turn_bank(m))
+            for m in GRAM_PAIRS:
+                if gram_step(m) == i:
+                    gram_products(m)
             if i == BIAS_BANK_STEP:
                 for h in range(HALVES):
-                    bias_bank.append(bank(6 + h))
+                    bias_bank.append(bank(4 + h))
                     nc.tensor.matmul(out=bias_bank[h][:], lhsT=ident_bf[:], rhs=bias_bf[:, halves[h]], start=True, stop=True)
-            for m in range(HEAD_PAIRS, PAIRS):
-                if m % 2 == 1 and turn_step(m) + 2 == i:
-                    quantise(groups[m // 2], x_codes, x_scales, m // 2)
-                if m >= GRAM_FIRST and turn_step(m) + 3 == i:
+            for m in GRAM_PAIRS:
+                if gram_step(m) + 1 == i:
                     gram_diagonals(m)
-            if 0 <= i < TOKEN_TILES:
+            for g in range(1, TOKEN_TILES // GROUP):
+                if quantise_step(g) == i:
+                    quantise(x_t, x_codes, x_scales, g)
+            if i >= 0:
                 stage_c(i)
-            if 0 <= i + 2 < TOKEN_TILES:
+            for m in VECTOR_COPIES:
+                if turn_step(m) == i:
+                    regroup("x", x_t, m, False)
+            if i + 2 <= last:
                 stage_a(i + 2)
-            if 0 <= i - 1 < TOKEN_TILES:
+            if i >= 1:
                 stage_d(i - 1)
-            if 0 <= i + 1 < TOKEN_TILES:
+            if i >= -1:
                 stage_b(i + 1)
-            for m in range(HEAD_PAIRS, PAIRS):
-                if turn_step(m) + 1 == i:
-                    if m % 2 == 0:
-                        groups[m // 2] = new_group()
-                    regroup(turned[m], groups[m // 2], m % 2, on_scalar=True)
-            for j in SQUARE_STEP.get(i, []):
-                square_sum(x_sb, j, x_sq)
-            if 0 <= i - 2 < TOKEN_TILES:
+            for j in range(1, TOKEN_TILES):
+                if j // 2 not in GRAM_PAIRS and square_step(j) == i:
+                    square_sum(x_sb, j, x_sq)
+            for m in range(4, PAIRS):
+                if turn_step(m) == i and m not in VECTOR_COPIES:
+                    regroup("x", x_t, m, True)
+            if i >= 2:
                 stage_e(i - 2)
+                store_tile(i - 2)
+
+        stage_c(last)
+        stage_d(last - 1)
+        stage_e(last - 2)
+        stage_d(last)
+        stage_e_vector(last - 1)
+        store_tile(last - 2)
+        stage_e_vector(last)

@@ -212,11 +212,14 @@ def tile_yatdense_t_kernel(tc, x, weight, alpha, bias, out):
         def stage_c(k):
             t[k] = work.tile([P, FEATS], F32, name="t")
             for h in range(HALVES):
-                nc.vector.tensor_tensor(out=t[k][:, halves[h]], in0=y[k][h][:], in1=q[k][:, halves[h]], op=ALU.mult)
+                nc.vector.scalar_tensor_tensor(
+                    out=t[k][:, halves[h]], in0=y[k][h][:], scalar=sigma[:, 0:1], in1=q[k][:, halves[h]],
+                    op0=ALU.mult, op1=ALU.mult,
+                )
 
         def stage_d(k):
             sq[k] = work.tile([P, FEATS], F32, name="sq")
-            nc.scalar.activation(out=sq[k][:], in_=t[k][:], func=ACT.Square, scale=sigma[:, 0:1])
+            nc.scalar.activation(out=sq[k][:], in_=t[k][:], func=ACT.Square)
 
         def stage_e(k):
             o[k] = store.tile([P, FEATS], F32, name="o")

@@ -71,7 +71,6 @@ def tile_yatdense_t_kernel(tc, x, weight, alpha, bias, out):
         work = ctx.enter_context(tc.tile_pool(name="work", bufs=3))
         store = ctx.enter_context(tc.tile_pool(name="store", bufs=4))
         psum = ctx.enter_context(tc.psum_pool(name="psum", bufs=1))
-        ctx.enter_context(tc.manual_schedule())
 
         def bank(n):
             return psum.tile([P, BANK], F32, name="bank%d" % n)
@@ -212,14 +211,11 @@ def tile_yatdense_t_kernel(tc, x, weight, alpha, bias, out):
         def stage_c(k):
             t[k] = work.tile([P, FEATS], F32, name="t")
             for h in range(HALVES):
-                nc.vector.scalar_tensor_tensor(
-                    out=t[k][:, halves[h]], in0=y[k][h][:], scalar=sigma[:, 0:1], in1=q[k][:, halves[h]],
-                    op0=ALU.mult, op1=ALU.mult,
-                )
+                nc.vector.tensor_tensor(out=t[k][:, halves[h]], in0=y[k][h][:], in1=q[k][:, halves[h]], op=ALU.mult)
 
         def stage_d(k):
             sq[k] = work.tile([P, FEATS], F32, name="sq")
-            nc.scalar.activation(out=sq[k][:], in_=t[k][:], func=ACT.Square)
+            nc.scalar.activation(out=sq[k][:], in_=t[k][:], func=ACT.Square, scale=sigma[:, 0:1])
 
         def stage_e(k):
             o[k] = store.tile([P, FEATS], F32, name="o")

import math
from contextlib import ExitStack

import concourse.mybir as mybir
from concourse.masks import make_identity

F32 = mybir.dt.float32
BF16 = mybir.dt.bfloat16
U32 = mybir.dt.uint32
U8 = mybir.dt.uint8
FP8X4 = mybir.dt.float8_e4m3fn_x4
ALU = mybir.AluOpType
ACT = mybir.ActivationFunctionType

P = 128
PACK = 4
TOKENS = 4096
K = 512
FEATS = 1024
TOKEN_TILES = TOKENS // P
FEAT_TILES = FEATS // P
PAIRS = TOKEN_TILES // 2
BANK = 512
HALVES = FEATS // BANK
GROUP = 4
EPS = 1e-6
ROOT_OF_BASE = math.sqrt(math.sqrt(FEATS) / math.log(1.0 + FEATS))

FLOPS = 2 * TOKENS * K * FEATS

FIRST_STEP = -2
VECTOR_TAIL = 2
GRAM_PAIRS = range(3, 14)
VECTOR_COPIES = (12, 14)
BIAS_BANK_STEP = 26


def turn_step(m):
    return m // 2 - 4


def turn_bank(m):
    return m - 2 if m < 6 else 4 + m % 2


def quantise_step(g):
    return g - 2


def gram_step(m):
    return max(m + 1, 2 * m - 4)


def square_step(j):
    return j - 3 if j < 6 else 2 * (j - 23)


def product_bank(k, h):
    return (6, 0, 2)[k % 3] + h


def tile_yatdense_t_kernel(tc, x, weight, alpha, bias, out):
    nc = tc.nc
    x_view = x.flatten_outer_dims().rearrange("(p j) k -> p (j k)", j=TOKEN_TILES)
    out_view = out.flatten_outer_dims().rearrange("(p j) n -> p j n", j=TOKEN_TILES)
    w_view = weight.rearrange("(i p) k -> p i k", p=P)

    with ExitStack() as ctx:
        keep = ctx.enter_context(tc.tile_pool(name="keep", bufs=1))
        stage = ctx.enter_context(tc.tile_pool(name="stage", bufs=3))
        work = ctx.enter_context(tc.tile_pool(name="work", bufs=3))
        store = ctx.enter_context(tc.tile_pool(name="store", bufs=4))
        psum = ctx.enter_context(tc.psum_pool(name="psum", bufs=1))

        def bank(n):
            return psum.tile([P, BANK], F32, name="bank%d" % n)

        w_sb = keep.tile([P, FEAT_TILES * K], BF16)
        x_sb = keep.tile([P, TOKEN_TILES * K], BF16)
        alpha_bf = keep.tile([P, 1], BF16)
        bias_bf = keep.tile([P, FEATS], BF16)

        def load_x(first, last):
            nc.sync.dma_start(out=x_sb[:, first * K : last * K], in_=x_view[:, first * K : last * K])

        for first, last in ((0, 2), (2, 4), (4, 8)):
            nc.sync.dma_start(
                out=w_sb[:, first * K : last * K].rearrange("p (i k) -> p i k", k=K), in_=w_view[:, first:last, :]
            )
        load_x(0, 4)
        nc.sync.dma_start(out=alpha_bf[:], in_=alpha.partition_broadcast(P))
        load_x(4, 8)
        load_x(8, 16)
        load_x(16, 24)
        load_x(24, 32)
        nc.sync.dma_start(out=bias_bf[:], in_=bias.partition_broadcast(P))

        ident = keep.tile([P, P], F32)
        make_identity(nc, ident[:])
        ident_bf = keep.tile([P, P], BF16)
        make_identity(nc, ident_bf[:])

        one = keep.tile([P, 1], F32)
        nc.vector.memset(one[:], 1.0)
        warm = keep.tile([P, 1], F32)
        nc.scalar.activation(out=warm[:], in_=one[:], func=ACT.Abs_reciprocal_sqrt)

        w_t = keep.tile([P, FEAT_TILES * K], BF16, align_bytes=64)
        x_t = keep.tile([P, TOKEN_TILES * K], BF16, align_bytes=64)
        w_codes = keep.tile([P, FEATS], U32, align_bytes=64)
        w_scales = keep.tile([P, FEATS], U8, align_bytes=64)
        x_codes = keep.tile([P, TOKENS], U32, align_bytes=64)
        x_scales = keep.tile([P, TOKENS], U8, align_bytes=64)
        w_sq = keep.tile([P, FEAT_TILES], F32)
        x_sq = keep.tile([P, TOKEN_TILES], F32)
        x_sq_gram = keep.tile([P, TOKEN_TILES], F32)
        w_sq_rows = keep.tile([P, FEATS], F32)
        sigma = keep.tile([P, 1], F32)
        halves = [slice(h * BANK, (h + 1) * BANK) for h in range(HALVES)]

        turned = {}

        def turn(name, src, m, n):
            turned[name, m] = bank(n)
            view = turned[name, m][:].rearrange("p (j u r) -> p j u r", j=2, u=2)
            words = src[:].bitcast(F32)
            for jj in range(2):
                for u in range(2):
                    c0 = (2 * m + jj) * (K // 2) + u * P
                    nc.tensor.transpose(view[:, jj, u, :], words[:, c0 : c0 + P], ident[:])

        def regroup(name, dst, m, on_scalar):
            to = dst[:].bitcast(F32).rearrange("p (j r u) -> p j r u", r=P, u=2)[:, 2 * m : 2 * m + 2, :, :]
            src = turned[name, m][:].rearrange("p (j u r) -> p j r u", j=2, u=2)
            if on_scalar:
                nc.scalar.copy(out=to, in_=src)
            else:
                nc.vector.tensor_copy(out=to, in_=src)

        def quantise(src, codes, scales, g):
            cols = slice(g * GROUP * P, (g + 1) * GROUP * P)
            nc.vector.quantize_mx(
                out=codes[:, cols].bitcast(FP8X4),
                scales=scales[:, cols],
                in_=src[:, g * GROUP * K : (g + 1) * GROUP * K],
            )

        def square_sum(src, j, dst):
            junk = stage.tile([P, K], BF16, name="junk")
            nc.scalar.activation(out=junk[:], in_=src[:, j * K : (j + 1) * K], func=ACT.Square, accum_out=dst[:, j : j + 1])

        y = {}
        e = {}
        q = {}
        t = {}
        sq = {}
        o = {}
        gram = {}
        bias_bank = []

        def multiply(k):
            rows = slice(k * P, (k + 1) * P)
            y[k] = []
            for h in range(HALVES):
                product = bank(product_bank(k, h))
                nc.tensor.matmul_mx(
                    out=product[:],
                    lhsT=x_codes[:, rows].bitcast(FP8X4),
                    lhsT_scale=x_scales[:, rows],
                    rhs=w_codes[:, halves[h]].bitcast(FP8X4),
                    rhs_scale=w_scales[:, halves[h]],
                    start=True,
                    stop=True,
                )
                y[k].append(product)

        def gram_products(m):
            gram[m] = bank(4 + m % 2)
            view = x_t[:].rearrange("p (j r t) -> p j r t", r=P, t=PACK)
            for jj in range(2):
                for tt in range(PACK):
                    operand = view[:, 2 * m + jj, :, tt]
                    nc.tensor.matmul(
                        out=gram[m][:, jj * P : (jj + 1) * P], lhsT=operand, rhs=operand,
                        start=(tt == 0), stop=(tt == PACK - 1),
                    )

        def gram_diagonals(m):
            for jj in range(2):
                masked = stage.tile([P, P], F32, name="masked")
                nc.vector.scalar_tensor_tensor(
                    out=masked[:], in0=gram[m][:, jj * P : (jj + 1) * P], scalar=1.0, in1=ident[:],
                    op0=ALU.mult, op1=ALU.mult, accum_out=x_sq_gram[:, 2 * m + jj : 2 * m + jj + 1],
                )

        def stage_a(k):
            e[k] = work.tile([P, FEATS], F32, name="e")
            for h in range(HALVES):
                nc.vector.scalar_tensor_tensor(
                    out=e[k][:, halves[h]], in0=y[k][h][:], scalar=-2.0, in1=w_sq_rows[:, halves[h]],
                    op0=ALU.mult, op1=ALU.add,
                )

        def stage_b(k):
            q[k] = work.tile([P, FEATS], F32, name="q")
            nc.scalar.activation(
                out=q[k][:], in_=e[k][:], func=ACT.Abs_reciprocal_sqrt,
                bias=(x_sq_gram if k // 2 in GRAM_PAIRS else x_sq)[:, k : k + 1], scale=1.0,
            )

        def stage_c(k):
            t[k] = work.tile([P, FEATS], F32, name="t")
            for h in range(HALVES):
                nc.vector.tensor_tensor(out=t[k][:, halves[h]], in0=y[k][h][:], in1=q[k][:, halves[h]], op=ALU.mult)

        def stage_d(k):
            sq[k] = work.tile([P, FEATS], F32, name="sq")
            nc.scalar.activation(out=sq[k][:], in_=t[k][:], func=ACT.Square, scale=sigma[:, 0:1])

        def stage_e(k):
            o[k] = store.tile([P, FEATS], F32, name="o")
            nc.gpsimd.tensor_tensor(out=o[k][:], in0=sq[k][:], in1=bias_bf[:], op=ALU.add)

        def store_tile(k):
            nc.sync.dma_start(out=out_view[:, k, :], in_=o[k][:])

        def stage_e_vector(k):
            o[k] = store.tile([P, FEATS], F32, name="o")
            for h in range(HALVES):
                nc.vector.tensor_tensor(out=o[k][:, halves[h]], in0=sq[k][:, halves[h]], in1=bias_bank[h][:], op=ALU.add)
                nc.sync.dma_start(out=out_view[:, k, halves[h]], in_=o[k][:, halves[h]])

        turn("w", w_sb, 0, 0)
        turn("w", w_sb, 1, 1)
        for i in range(4):
            square_sum(w_sb, i, w_sq)
        regroup("w", w_t, 0, False)
        regroup("w", w_t, 1, False)
        turn("w", w_sb, 2, 2)
        turn("w", w_sb, 3, 3)
        for i in range(4, FEAT_TILES):
            square_sum(w_sb, i, w_sq)
        quantise(w_t, w_codes, w_scales, 0)
        regroup("w", w_t, 2, False)
        regroup("w", w_t, 3, False)
        turn("x", x_sb, 0, 4)
        turn("x", x_sb, 1, 5)
        regroup("x", x_t, 0, False)
        quantise(w_t, w_codes, w_scales, 1)
        regroup("x", x_t, 1, False)
        turn("x", x_sb, 2, 6)
        turn("x", x_sb, 3, 7)
        spread = [bank(0), bank(1)]
        for i in range(FEAT_TILES):
            nc.tensor.transpose(
                spread[i // 4][:, (i % 4) * P : (i % 4 + 1) * P], w_sq[:, i : i + 1].to_broadcast([P, P]), ident[:]
            )
        square_sum(x_sb, 0, x_sq)
        regroup("x", x_t, 2, True)
        regroup("x", x_t, 3, True)
        quantise(x_t, x_codes, x_scales, 0)
        for h in range(HALVES):
            nc.vector.tensor_scalar_add(out=w_sq_rows[:, halves[h]], in0=spread[h][:], scalar1=EPS)

        alpha_f = keep.tile([P, 1], F32)
        nc.gpsimd.tensor_copy(out=alpha_f[:], in_=alpha_bf[:])
        root = keep.tile([P, 1], F32)
        nc.gpsimd.tensor_scalar(
            out=root[:], in0=alpha_f[:], scalar1=0.0, scalar2=ROOT_OF_BASE, op0=ALU.mult, op1=ALU.add
        )
        nc.gpsimd.tensor_tensor(out=sigma[:], in0=root[:], in1=alpha_f[:], op=ALU.pow)

        last = TOKEN_TILES - 1
        for i in range(FIRST_STEP, last):
            if i + 2 <= last:
                multiply(i + 2)
            for m in range(4, PAIRS):
                if turn_step(m) == i:
                    turn("x", x_sb, m, turn_bank(m))
            for m in GRAM_PAIRS:
                if gram_step(m) == i:
                    gram_products(m)
            if i == BIAS_BANK_STEP:
                for h in range(HALVES):
                    bias_bank.append(bank(4 + h))
                    nc.tensor.matmul(out=bias_bank[h][:], lhsT=ident_bf[:], rhs=bias_bf[:, halves[h]], start=True, stop=True)
            for m in GRAM_PAIRS:
                if gram_step(m) + 1 == i:
                    gram_diagonals(m)
            for g in range(1, TOKEN_TILES // GROUP):
                if quantise_step(g) == i:
                    quantise(x_t, x_codes, x_scales, g)
            if i >= 0:
                stage_c(i)
            for m in VECTOR_COPIES:
                if turn_step(m) == i:
                    regroup("x", x_t, m, False)
            if i + 2 <= last:
                stage_a(i + 2)
            if i >= 1:
                stage_d(i - 1)
            if i >= -1:
                stage_b(i + 1)
            for j in range(1, TOKEN_TILES):
                if j // 2 not in GRAM_PAIRS and square_step(j) == i:
                    square_sum(x_sb, j, x_sq)
            for m in range(4, PAIRS):
                if turn_step(m) == i and m not in VECTOR_COPIES:
                    regroup("x", x_t, m, True)
            if i >= 2:
                stage_e(i - 2)
                store_tile(i - 2)

        stage_c(last)
        stage_d(last - 1)
        stage_e(last - 2)
        stage_d(last)
        stage_e_vector(last - 1)
        store_tile(last - 2)
        stage_e_vector(last)
